import numpy as np
import ml_dtypes


def mxq(x, axis, fmt="e4m3"):
    dtype, down = {"e4m3": (ml_dtypes.float8_e4m3fn, 7), "e5m2": (ml_dtypes.float8_e5m2, 14)}[fmt]
    v = np.moveaxis(np.asarray(x, np.float32).astype(ml_dtypes.bfloat16).astype(np.float64), axis, -1)
    blocks = v.reshape(v.shape[:-1] + (-1, 32))
    amax = np.abs(blocks).max(-1, keepdims=True)
    byte = np.maximum(np.where(amax > 0, np.frexp(amax)[1] - 1 + 127, 0) - down, 1)
    scale = np.exp2(byte - 127.0)
    codes = (blocks / scale).astype(np.float32).astype(dtype).astype(np.float64)
    return np.moveaxis((codes * scale).reshape(v.shape), -1, axis)


WIDE = False


def mx_kscale(k):
    if not WIDE:
        return np.ones(k)
    levels = np.array([10, -10, 5, -5, 0])
    if k % 512:
        return np.exp2(np.random.permutation(np.resize(levels, k // 32))).repeat(32)
    a = np.empty((k // 512, 16))
    for p in range(k // 512):
        a[p, :8] = np.random.permutation(np.resize(levels, 8))
        for g in range(8):
            far = levels[np.abs(levels - a[p, g]) >= 10]
            a[p, g + 8] = far[np.random.randint(len(far))]
    return np.exp2(a.ravel()).repeat(32)


BF16 = ml_dtypes.bfloat16


def bf(x):
    return np.asarray(x, np.float32).astype(BF16)


def f64(x):
    return np.asarray(x).astype(np.float64)


B, F, G, N, L = 64, 512, 128, 100, 7
S2 = (L + 1) ** 2


def draw0():
    s = mx_kscale(F)
    return {"x": bf(np.random.standard_normal((B, F, S2)) * s[None, :, None]),
            "psi": bf(np.random.standard_normal((G, F, S2)) / s[None, :, None])}


def core(x, psi):
    xq = mxq(f64(x), 1, "e4m3")
    pq = mxq(f64(psi), 1, "e4m3")
    scale = 1.0 / np.sqrt(F)
    outs = []
    for l in range(L + 1):
        s, d = l * l, 2 * l + 1
        a = xq[:, :, s:s + d].transpose(0, 2, 1).reshape(B * d, F)
        p = pq[:, :, s:s + d].transpose(1, 0, 2).reshape(F, G * d)
        o = scale * (a @ p)
        outs.append(o.reshape(B, d, G, d).transpose(2, 0, 1, 3).reshape(G, B, d * d))
    return np.concatenate(outs, axis=-1)


def e4m3fn_bytes(y):
    return np.clip(np.asarray(y, np.float64), -448.0, 448.0).astype(np.float32).astype(ml_dtypes.float8_e4m3fn).view(np.uint8)


def e4m3fn_values(b):
    return np.asarray(b, np.uint8).view(ml_dtypes.float8_e4m3fn).astype(np.float64)


def setup_inputs():
    d = draw0()
    x0 = np.asarray(d['psi']).astype(np.float64)
    s = (np.max(np.abs(x0), axis=(0, 2), keepdims=True) / 448.0).astype(np.float32)
    out = {}
    for k, v in d.items():
        if k == 'psi':
            out['psi_bytes'] = e4m3fn_bytes(x0 / s.astype(np.float64))
            out['psi_scale'] = s
        else:
            out[k] = v
    return out


def reference(x, psi_bytes, psi_scale):
    return core(x, e4m3fn_values(psi_bytes) * psi_scale.astype(np.float64))

@@ -1,0 +1,216 @@
+from contextlib import ExitStack
+
+import concourse.mybir as mybir
+
+B, F, G, S2, L = 64, 512, 128, 64, 7
+OUTW = 680
+FLOPS = 2 * F * G * B * OUTW
+
+F32 = mybir.dt.float32
+BF16 = mybir.dt.bfloat16
+U32 = mybir.dt.uint32
+U8 = mybir.dt.uint8
+FP8 = mybir.dt.float8_e4m3fn
+FP8X4 = mybir.dt.float8_e4m3fn_x4
+COPY = mybir.ActivationFunctionType.Copy
+MULT = mybir.AluOpType.mult
+
+P = 128
+PACK = 4
+NB = 8
+N_CHUNKS = B // NB
+WIN = 16
+XCOLS = 72
+X_SEGMENTS = ((0, 0, 40), (36, 40, 16), (48, 56, 16))
+GT = 16
+N_TILES = G // GT
+OUT_SCALE = 1.0 / (F ** 0.5)
+VECTOR_BANKS = (10, 17)
+
+
+def make_blocks():
+    blocks = []
+    for l, win, row0 in ((7, 56, 1), (6, 40, 0), (5, 24, 1), (4, 16, 0)):
+        d = 2 * l + 1
+        nq = (d + 3) // 4
+        quads = tuple((tuple(min(l * l + 4 * j + mi, S2 - 1) for mi in range(4)), row0, row0 + d) for j in range(nq))
+        blocks.append((win, row0, d, 4 * nq, quads, ((l, 0),)))
+    blocks.append((0, 0, 16, 16, (((0, 1, 2, 3), 0, 4), ((4, 5, 6, 7), 4, 9), ((8, 9, 10, 11), 4, 16), ((12, 13, 14, 15), 9, 16)),
+                   ((0, 0), (1, 1), (2, 4), (3, 9))))
+    return blocks
+
+
+BLOCKS = make_blocks()
+R_OFFSETS = [sum(NB * b[2] * b[3] for b in BLOCKS[:i]) for i in range(len(BLOCKS) + 1)]
+OUT_OFFSETS = [sum((2 * k + 1) ** 2 for k in range(l)) for l in range(L + 1)]
+
+F_BYTES = NB * OUTW * 4
+PLANE_BYTES = G * PACK * 2
+PARTS = ((0, 16, 0), (16, 40, F_BYTES), (40, 64, F_BYTES + 24 * PLANE_BYTES))
+GROUPED_BYTES = F_BYTES + 48 * PLANE_BYTES
+RAW_BYTES = GT * PACK * S2
+W_BYTES = 2 * RAW_BYTES
+R_BYTES = 4 * R_OFFSETS[-1]
+OFF_RAW = GROUPED_BYTES
+OFF_W = OFF_RAW + 4 * RAW_BYTES
+OFF_R0 = OFF_W + 3 * W_BYTES
+assert F_BYTES <= 24 * PLANE_BYTES and R_BYTES <= OFF_R0 - OFF_RAW
+
+
+def tile_s2conv_pa_kernel(tc, x, psi_bytes, psi_scale, out):
+    nc = tc.nc
+    with ExitStack() as ctx:
+        keep = ctx.enter_context(tc.tile_pool(name="keep", bufs=1))
+        big = ctx.enter_context(tc.tile_pool(name="big", bufs=1))
+        xs = ctx.enter_context(tc.tile_pool(name="xs", bufs=3))
+        psum = ctx.enter_context(tc.psum_pool(name="psum", bufs=8))
+        ctx.enter_context(tc.manual_schedule())
+
+        scale_sb = keep.tile([P, PACK], F32, name="scale_sb")
+        psi_codes = keep.tile([P, S2, G], U32, name="psi_codes", align_bytes=64)
+        psi_scl = keep.tile([P, S2, G], U8, name="psi_scl", align_bytes=64)
+        x_raw = keep.tile([P, B, PACK, S2], BF16, name="x_raw")
+
+        parts = [big.tile([P, hi - lo, G, PACK], BF16, name="grouped%d" % lo, align_bytes=64, offset=off) for lo, hi, off in PARTS]
+        raws = [big.tile([P, GT, PACK, S2], U8, name="raw%d" % i, align_bytes=64, offset=OFF_RAW + i * RAW_BYTES) for i in range(4)]
+        ws = [big.tile([P, GT, PACK, S2], BF16, name="w%d" % i, align_bytes=64, offset=OFF_W + i * W_BYTES) for i in range(3)]
+
+        psi_view = psi_bytes.rearrange("g (p t) c -> p g t c", t=PACK)
+        x_view = x.rearrange("b (p t) c -> p b t c", t=PACK)
+
+        def load_psi(j):
+            nc.sync.dma_start(out=raws[j % 4][:], in_=psi_view[:, j * GT:(j + 1) * GT])
+
+        def cast(j):
+            src = raws[j % 4][:].rearrange("p g t c -> p (g t c)").bitcast(FP8)
+            dst = ws[j % 3][:].rearrange("p g t c -> p (g t c)")
+            if j == 1:
+                nc.vector.tensor_copy(out=dst, in_=src)
+            elif j == 2:
+                nc.scalar.activation(out=dst, in_=src, func=COPY)
+            else:
+                nc.scalar.copy(out=dst, in_=src)
+
+        def scale_and_permute(j):
+            w = ws[j % 3]
+            for t in range(PACK):
+                nc.vector.tensor_scalar(out=w[:, :, t, :], in0=w[:, :, t, :], scalar1=scale_sb[:, t:t + 1], scalar2=None, op0=MULT)
+            for part, (lo, hi, off) in zip(parts, PARTS):
+                nc.vector.tensor_copy(
+                    out=part[:, :, j * GT:(j + 1) * GT, :].rearrange("p (cb i) g t -> p cb g t i", i=4),
+                    in_=w[:, :, :, lo:hi].rearrange("p g t (cb i) -> p cb g t i", i=4),
+                )
+
+        def quantize_psi(q):
+            pi = 0 if q < 2 else (1 if q < 5 else 2)
+            nc.vector.quantize_mx(
+                out=psi_codes[:, 8 * q:8 * (q + 1), :].rearrange("p c g -> p (c g)").bitcast(FP8X4),
+                scales=psi_scl[:, 8 * q:8 * (q + 1), :].rearrange("p c g -> p (c g)"),
+                in_=parts[pi][:, 8 * q - PARTS[pi][0]:8 * (q + 1) - PARTS[pi][0]].rearrange("p c g t -> p (c g t)"),
+            )
+
+        x_tiles = {}
+
+        def permute_x(k, engine):
+            xg = xs.tile([P, XCOLS, NB, PACK], BF16, name="xg", align_bytes=64)
+            for c0, col0, n in X_SEGMENTS:
+                dst = xg[:, col0:col0 + n].rearrange("p (cb i) b t -> p cb b t i", i=4)
+                src = x_raw[:, k * NB:(k + 1) * NB, :, c0:c0 + n].rearrange("p b t (cb i) -> p cb b t i", i=4)
+                if engine == "scalar":
+                    nc.scalar.copy(out=dst, in_=src)
+                else:
+                    nc.vector.tensor_copy(out=dst, in_=src)
+            x_tiles[k] = xg
+
+        def quantize_x(k):
+            xg = x_tiles[k]
+            xc = xs.tile([P, XCOLS * NB], U32, name="xc", align_bytes=64)
+            xsc = xs.tile([P, XCOLS * NB], U8, name="xsc", align_bytes=64)
+            flat = xg[:].rearrange("p c b t -> p (c b t)")
+            for w0, wn in ((0, 512), (512, 64)):
+                nc.vector.quantize_mx(
+                    out=xc[:, w0:w0 + wn].bitcast(FP8X4),
+                    scales=xsc[:, w0:w0 + wn],
+                    in_=flat[:, PACK * w0:PACK * (w0 + wn)],
+                )
+            x_tiles[k] = (xc, xsc)
+
+        nc.sync.dma_start(out=scale_sb[:], in_=psi_scale.rearrange("o (p t) z -> p (o t z)", t=PACK))
+        for j in range(4):
+            load_psi(j)
+        for j in range(N_TILES):
+            cast(j)
+            if j + 4 < N_TILES:
+                load_psi(j + 4)
+            if j == 3:
+                for h in range(4):
+                    nc.sync.dma_start(out=x_raw[:, 16 * h:16 * (h + 1)], in_=x_view[:, 16 * h:16 * (h + 1)])
+            if j >= 1:
+                scale_and_permute(j - 1)
+        permute_x(0, "scalar")
+        permute_x(1, "scalar")
+        scale_and_permute(N_TILES - 1)
+        quantize_x(0)
+        quantize_psi(7)
+        quantize_psi(6)
+        quantize_x(1)
+        late_quantize = [5, 4, 3, 2, 1, 0]
+
+        rs = [big.tile([P, R_OFFSETS[-1]], F32, name="r0", align_bytes=64, offset=OFF_R0),
+              big.tile([P, R_OFFSETS[-1]], F32, name="r1", align_bytes=64, offset=OFF_RAW)]
+        fs = [big.tile([P, NB, OUTW], F32, name="f%d" % i, align_bytes=64, offset=PARTS[i][2]) for i in range(3)]
+
+        def rblock(k, bi):
+            return rs[k % 2][:, R_OFFSETS[bi]:R_OFFSETS[bi + 1]].rearrange("p (b u m) -> p b u m", b=NB, m=BLOCKS[bi][3])
+
+        def compact(k, bi):
+            for l, r0 in BLOCKS[bi][5]:
+                d = 2 * l + 1
+                cl = OUT_OFFSETS[l]
+                nc.vector.tensor_copy(
+                    out=fs[(2 - k) % 3][:, :, cl:cl + d * d].rearrange("p b (u m) -> p b u m", m=d),
+                    in_=rblock(k, bi)[:, :, r0:r0 + d, r0:r0 + d],
+                )
+
+        def store(k):
+            nc.sync.dma_start(out=out[:, k * NB:(k + 1) * NB, :], in_=fs[(2 - k) % 3][:])
+
+        for k in range(N_CHUNKS):
+            xc, xsc = x_tiles[k]
+            bank = 0
+            for bi, (win, row0, rows, pitch, quads, degrees) in enumerate(BLOCKS):
+                for j, (stat, lo, hi) in enumerate(quads):
+                    pt = psum.tile([P, 4, WIN * NB], F32, name="pt")
+                    for mi, c in enumerate(stat):
+                        nc.tensor.matmul_mx(
+                            out=pt[:, mi, :],
+                            lhsT=psi_codes[:, c, :].bitcast(FP8X4),
+                            lhsT_scale=psi_scl[:, c, :],
+                            rhs=xc[:, win * NB:(win + WIN) * NB].bitcast(FP8X4),
+                            rhs_scale=xsc[:, win * NB:(win + WIN) * NB],
+                            start=True,
+                            stop=True,
+                        )
+                    src = pt[:, :, lo * NB:hi * NB].rearrange("p m (u b) -> p b u m", b=NB)
+                    dst = rblock(k, bi)[:, :, lo - row0:hi - row0, 4 * j:4 * j + 4]
+                    if bank in VECTOR_BANKS and k > 0:
+                        nc.vector.tensor_scalar(out=dst, in0=src, scalar1=OUT_SCALE, scalar2=None, op0=MULT)
+                    else:
+                        nc.scalar.activation(out=dst, in_=src, func=COPY, scale=OUT_SCALE)
+                    bank += 1
+                if k == 0:
+                    for q in late_quantize[:(2, 1, 1, 2, 0)[bi]]:
+                        quantize_psi(q)
+                    late_quantize = late_quantize[(2, 1, 1, 2, 0)[bi]:]
+                if bi == 0:
+                    if k > 0:
+                        compact(k - 1, len(BLOCKS) - 1)
+                        store(k - 1)
+                    if k + 2 < N_CHUNKS:
+                        permute_x(k + 2, "vector")
+                else:
+                    compact(k, bi - 1)
+                    if bi == 1 and k + 2 < N_CHUNKS:
+                        quantize_x(k + 2)
+        compact(N_CHUNKS - 1, len(BLOCKS) - 1)
+        store(N_CHUNKS - 1)

@@ -17,44 +17,67 @@ MULT = mybir.AluOpType.mult
 
 P = 128
 PACK = 4
-NB = 8
-N_CHUNKS = B // NB
-WIN = 16
-XCOLS = 72
-X_SEGMENTS = ((0, 0, 40), (36, 40, 16), (48, 56, 16))
+HB = 32
 GT = 16
 N_TILES = G // GT
+QC = 16
 OUT_SCALE = 1.0 / (F ** 0.5)
-VECTOR_BANKS = (10, 17)
+
+GROUPS = ((114, 169, 48), (72, 113, 36), (42, 71, 25), (21, 41, 16), (0, 20, 0))
+PIECES = ((114, 56), (72, 42), (0, 72))
+GROUP_PIECE = (0, 1, 2, 2, 2)
+STAGES = ((0, 0), (0, 1), (1, 0), (1, 1), (2, 0), (3, 0), (4, 0), (2, 1), (3, 1), (4, 1))
+VECTOR_FROM_STAGE = 7
 
 
-def make_blocks():
-    blocks = []
-    for l, win, row0 in ((7, 56, 1), (6, 40, 0), (5, 24, 1), (4, 16, 0)):
+def make_words():
+    words = []
+    for l in range(L + 1):
         d = 2 * l + 1
-        nq = (d + 3) // 4
-        quads = tuple((tuple(min(l * l + 4 * j + mi, S2 - 1) for mi in range(4)), row0, row0 + d) for j in range(nq))
-        blocks.append((win, row0, d, 4 * nq, quads, ((l, 0),)))
-    blocks.append((0, 0, 16, 16, (((0, 1, 2, 3), 0, 4), ((4, 5, 6, 7), 4, 9), ((8, 9, 10, 11), 4, 16), ((12, 13, 14, 15), 9, 16)),
-                   ((0, 0), (1, 1), (2, 4), (3, 9))))
-    return blocks
+        for u in range(d):
+            for m in range(d):
+                words.append((l * l + m, l * l + u, d))
+    return words
 
 
-BLOCKS = make_blocks()
-R_OFFSETS = [sum(NB * b[2] * b[3] for b in BLOCKS[:i]) for i in range(len(BLOCKS) + 1)]
-OUT_OFFSETS = [sum((2 * k + 1) ** 2 for k in range(l)) for l in range(L + 1)]
+WORDS = make_words()
 
-F_BYTES = NB * OUTW * 4
-PLANE_BYTES = G * PACK * 2
-PARTS = ((0, 16, 0), (16, 40, F_BYTES), (40, 64, F_BYTES + 24 * PLANE_BYTES))
-GROUPED_BYTES = F_BYTES + 48 * PLANE_BYTES
+
+def make_jobs(first, last, base):
+    jobs = []
+    taken = set()
+    for line in range(first, last + 1):
+        if line in taken:
+            continue
+        quad = WORDS[4 * line:4 * line + 4]
+        step = quad[0][2]
+        count = 1
+        while line + count * step <= last:
+            later = WORDS[4 * (line + count * step):4 * (line + count * step) + 4]
+            if all(a[0] == b[0] and b[1] == a[1] + 4 * count for a, b in zip(quad, later)):
+                count += 1
+            else:
+                break
+        for j in range(count):
+            taken.add(line + j * step)
+        first_slot = (quad[0][1] - base) // 4
+        passes = tuple((q[0], (q[1] - base) % 4, (q[1] - base) // 4 - first_slot) for q in quad)
+        jobs.append((line, step, count, first_slot, passes))
+    return jobs
+
+
+JOBS = [make_jobs(first, last, base) for first, last, base in GROUPS]
+
+O7_BYTES = PIECES[0][1] * 4 * HB * 4
+O6_BYTES = PIECES[1][1] * 4 * HB * 4
+OB_BYTES = PIECES[2][1] * 4 * HB * 4
 RAW_BYTES = GT * PACK * S2
-W_BYTES = 2 * RAW_BYTES
-R_BYTES = 4 * R_OFFSETS[-1]
-OFF_RAW = GROUPED_BYTES
-OFF_W = OFF_RAW + 4 * RAW_BYTES
-OFF_R0 = OFF_W + 3 * W_BYTES
-assert F_BYTES <= 24 * PLANE_BYTES and R_BYTES <= OFF_R0 - OFF_RAW
+W_BYTES = G * PACK * S2 * 2
+GROUPED_BYTES = QC * G * PACK * 2
+OFF_W = 2 * O7_BYTES
+OFF_GROUPED = OFF_W + W_BYTES
+PIECE_OFFSETS = ((0, O7_BYTES), (0, O7_BYTES), (OFF_W, OFF_W + OB_BYTES))
+assert N_TILES * RAW_BYTES <= 2 * O7_BYTES and O6_BYTES <= O7_BYTES and 2 * OB_BYTES <= W_BYTES + GROUPED_BYTES
 
 
 def tile_s2conv_pa_kernel(tc, x, psi_bytes, psi_scale, out):
@@ -62,155 +85,157 @@ def tile_s2conv_pa_kernel(tc, x, psi_bytes, psi_scale, out):
     with ExitStack() as ctx:
         keep = ctx.enter_context(tc.tile_pool(name="keep", bufs=1))
         big = ctx.enter_context(tc.tile_pool(name="big", bufs=1))
-        xs = ctx.enter_context(tc.tile_pool(name="xs", bufs=3))
+        xgs = ctx.enter_context(tc.tile_pool(name="xgs", bufs=2))
+        xcs = ctx.enter_context(tc.tile_pool(name="xcs", bufs=4))
         psum = ctx.enter_context(tc.psum_pool(name="psum", bufs=8))
         ctx.enter_context(tc.manual_schedule())
 
         scale_sb = keep.tile([P, PACK], F32, name="scale_sb")
         psi_codes = keep.tile([P, S2, G], U32, name="psi_codes", align_bytes=64)
         psi_scl = keep.tile([P, S2, G], U8, name="psi_scl", align_bytes=64)
-        x_raw = keep.tile([P, B, PACK, S2], BF16, name="x_raw")
+        x_raw = [keep.tile([P, HB, PACK, S2], BF16, name="x_raw%d" % h) for h in range(2)]
 
-        parts = [big.tile([P, hi - lo, G, PACK], BF16, name="grouped%d" % lo, align_bytes=64, offset=off) for lo, hi, off in PARTS]
-        raws = [big.tile([P, GT, PACK, S2], U8, name="raw%d" % i, align_bytes=64, offset=OFF_RAW + i * RAW_BYTES) for i in range(4)]
-        ws = [big.tile([P, GT, PACK, S2], BF16, name="w%d" % i, align_bytes=64, offset=OFF_W + i * W_BYTES) for i in range(3)]
+        raws = [big.tile([P, GT, PACK, S2], U8, name="raw%d" % j, align_bytes=64, offset=j * RAW_BYTES) for j in range(N_TILES)]
+        w = big.tile([P, G, PACK, S2], BF16, name="w", align_bytes=64, offset=OFF_W)
+        grouped = big.tile([P, QC, G, PACK], BF16, name="grouped", align_bytes=64, offset=OFF_GROUPED)
 
         psi_view = psi_bytes.rearrange("g (p t) c -> p g t c", t=PACK)
         x_view = x.rearrange("b (p t) c -> p b t c", t=PACK)
 
-        def load_psi(j):
-            nc.sync.dma_start(out=raws[j % 4][:], in_=psi_view[:, j * GT:(j + 1) * GT])
+        nc.sync.dma_start(out=scale_sb[:], in_=psi_scale.rearrange("o (p t) z -> p (o t z)", t=PACK))
+        for j in range(N_TILES):
+            nc.sync.dma_start(out=raws[j][:], in_=psi_view[:, j * GT:(j + 1) * GT])
+        for h in range(2):
+            for e in range(2):
+                nc.sync.dma_start(out=x_raw[h][:, 16 * e:16 * (e + 1)], in_=x_view[:, HB * h + 16 * e:HB * h + 16 * (e + 1)])
 
-        def cast(j):
-            src = raws[j % 4][:].rearrange("p g t c -> p (g t c)").bitcast(FP8)
-            dst = ws[j % 3][:].rearrange("p g t c -> p (g t c)")
-            if j == 1:
-                nc.vector.tensor_copy(out=dst, in_=src)
-            elif j == 2:
-                nc.scalar.activation(out=dst, in_=src, func=COPY)
-            else:
+        def cast(j, engine):
+            src = raws[j][:].rearrange("p g t c -> p (g t c)").bitcast(FP8)
+            dst = w[:, j * GT:(j + 1) * GT].rearrange("p g t c -> p (g t c)")
+            if engine == "scalar":
                 nc.scalar.copy(out=dst, in_=src)
+            else:
+                nc.vector.tensor_copy(out=dst, in_=src)
 
-        def scale_and_permute(j):
-            w = ws[j % 3]
+        def scale_quarter(q, g0, g1):
             for t in range(PACK):
-                nc.vector.tensor_scalar(out=w[:, :, t, :], in0=w[:, :, t, :], scalar1=scale_sb[:, t:t + 1], scalar2=None, op0=MULT)
-            for part, (lo, hi, off) in zip(parts, PARTS):
-                nc.vector.tensor_copy(
-                    out=part[:, :, j * GT:(j + 1) * GT, :].rearrange("p (cb i) g t -> p cb g t i", i=4),
-                    in_=w[:, :, :, lo:hi].rearrange("p g t (cb i) -> p cb g t i", i=4),
-                )
+                part = w[:, g0:g1, t, QC * q:QC * (q + 1)]
+                nc.vector.tensor_scalar(out=part, in0=part, scalar1=scale_sb[:, t:t + 1], scalar2=None, op0=MULT)
 
-        def quantize_psi(q):
-            pi = 0 if q < 2 else (1 if q < 5 else 2)
-            nc.vector.quantize_mx(
-                out=psi_codes[:, 8 * q:8 * (q + 1), :].rearrange("p c g -> p (c g)").bitcast(FP8X4),
-                scales=psi_scl[:, 8 * q:8 * (q + 1), :].rearrange("p c g -> p (c g)"),
-                in_=parts[pi][:, 8 * q - PARTS[pi][0]:8 * (q + 1) - PARTS[pi][0]].rearrange("p c g t -> p (c g t)"),
+        def permute_quarter(q, c0, c1, g0, g1):
+            nc.vector.tensor_copy(
+                out=grouped[:, c0:c1, g0:g1, :].rearrange("p (cb i) g t -> p cb g t i", i=4),
+                in_=w[:, g0:g1, :, QC * q + c0:QC * q + c1].rearrange("p g t (cb i) -> p cb g t i", i=4),
             )
 
-        x_tiles = {}
+        def quantize_quarter(q, e):
+            c0 = QC * q + 8 * e
+            nc.vector.quantize_mx(
+                out=psi_codes[:, c0:c0 + 8, :].rearrange("p c g -> p (c g)").bitcast(FP8X4),
+                scales=psi_scl[:, c0:c0 + 8, :].rearrange("p c g -> p (c g)"),
+                in_=grouped[:, 8 * e:8 * (e + 1)].rearrange("p c g t -> p (c g t)"),
+            )
 
-        def permute_x(k, engine):
-            xg = xs.tile([P, XCOLS, NB, PACK], BF16, name="xg", align_bytes=64)
-            for c0, col0, n in X_SEGMENTS:
-                dst = xg[:, col0:col0 + n].rearrange("p (cb i) b t -> p cb b t i", i=4)
-                src = x_raw[:, k * NB:(k + 1) * NB, :, c0:c0 + n].rearrange("p b t (cb i) -> p cb b t i", i=4)
-                if engine == "scalar":
-                    nc.scalar.copy(out=dst, in_=src)
+        x_grouped = {}
+        x_ready = {}
+
+        def permute_x(grp, h, engine):
+            base = GROUPS[grp][2]
+            xg = xgs.tile([P, 16, HB, PACK], BF16, name="xg", align_bytes=64)
+            dst = xg[:].rearrange("p (r j) b t -> p j b t r", r=4)
+            src = x_raw[h][:, :, :, base:base + 16].rearrange("p b t (j r) -> p j b t r", r=4)
+            if engine == "scalar":
+                nc.scalar.copy(out=dst, in_=src)
+            else:
+                nc.vector.tensor_copy(out=dst, in_=src)
+            x_grouped[(grp, h)] = xg
+
+        def quantize_x(grp, h):
+            xc = xcs.tile([P, 16 * HB], U32, name="xc", align_bytes=64)
+            xsc = xcs.tile([P, 16 * HB], U8, name="xsc", align_bytes=64)
+            nc.vector.quantize_mx(
+                out=xc[:].bitcast(FP8X4),
+                scales=xsc[:],
+                in_=x_grouped[(grp, h)][:].rearrange("p s b t -> p (s b t)"),
+            )
+            x_ready[(grp, h)] = (xc, xsc)
+
+        for pair in range(N_TILES // 2):
+            cast(2 * pair, "scalar")
+            cast(2 * pair + 1, "vector")
+            scale_quarter(3, 2 * GT * pair, 2 * GT * (pair + 1))
+            permute_quarter(3, 0, QC, 2 * GT * pair, 2 * GT * (pair + 1))
+        permute_x(0, 0, "scalar")
+        permute_x(0, 1, "scalar")
+        quantize_x(0, 0)
+        quantize_quarter(3, 0)
+        quantize_quarter(3, 1)
+        quantize_x(0, 1)
+
+        later = []
+
+        def add_quarter(q):
+            later.append((None, lambda: scale_quarter(q, 0, G)))
+            later.append((None, lambda: permute_quarter(q, 0, 8, 0, G)))
+            later.append((("permuted", q), lambda: permute_quarter(q, 8, QC, 0, G)))
+            later.append((None, lambda: quantize_quarter(q, 0)))
+            later.append((("quarter", q), lambda: quantize_quarter(q, 1)))
+
+        def add_x_pair(a, b):
+            later.append((None, lambda: permute_x(a[0], a[1], "vector")))
+            later.append((None, lambda: permute_x(b[0], b[1], "vector")))
+            later.append((("x", a), lambda: quantize_x(a[0], a[1])))
+            later.append((("x", b), lambda: quantize_x(b[0], b[1])))
+
+        add_quarter(2)
+        add_x_pair((1, 0), (1, 1))
+        add_quarter(1)
+        add_x_pair((2, 0), (3, 0))
+        add_quarter(0)
+        add_x_pair((4, 0), (2, 1))
+        add_x_pair((3, 1), (4, 1))
+        done = set()
+
+        def need(what):
+            while what not in done:
+                key, call = later[len(done)]
+                call()
+                done.add((len(done), key) if key is None else key)
+
+        NEEDS = {2: (("quarter", 2), ("x", (1, 0))), 3: (("x", (1, 1)),), 4: (("quarter", 1), ("x", (2, 0)), ("permuted", 0)),
+                 5: (("x", (3, 0)),), 6: (("quarter", 0), ("x", (4, 0))), 7: (("x", (2, 1)),), 8: (("x", (3, 1)),), 9: (("x", (4, 1)),)}
+
+        out_tiles = {}
+        for k, (grp, h) in enumerate(STAGES):
+            for what in NEEDS.get(k, ()):
+                need(what)
+            if k == VECTOR_FROM_STAGE:
+                need(("x", (4, 1)))
+            piece = GROUP_PIECE[grp]
+            line0, lines = PIECES[piece]
+            if (piece, h) not in out_tiles:
+                out_tiles[(piece, h)] = big.tile([P, HB, 4 * lines], F32, name="o%d%d" % (piece, h), align_bytes=64,
+                                                 offset=PIECE_OFFSETS[piece][h])
+            ot = out_tiles[(piece, h)]
+            xc, xsc = x_ready[(grp, h)]
+            for n, (line, step, count, first_slot, passes) in enumerate(JOBS[grp]):
+                pt = psum.tile([P, 512], F32, name="pt")
+                for f, (c, r, shift) in enumerate(passes):
+                    nc.tensor.matmul_mx(
+                        out=pt[:, 128 * f - HB * shift:128 * (f + 1) - HB * shift],
+                        lhsT=psi_codes[:, c, :].bitcast(FP8X4),
+                        lhsT_scale=psi_scl[:, c, :],
+                        rhs=xc[:, 128 * r:128 * (r + 1)].bitcast(FP8X4),
+                        rhs_scale=xsc[:, 128 * r:128 * (r + 1)],
+                        start=True,
+                        stop=True,
+                    )
+                src = pt[:].rearrange("p (f j b) -> p b j f", f=4, j=4)[:, :, first_slot:first_slot + count, :]
+                n0 = line - line0
+                dst = ot[:].rearrange("p b (n f) -> p b n f", f=4)[:, :, n0:n0 + step * (count - 1) + 1:step, :]
+                if k >= VECTOR_FROM_STAGE and n % 2 == 1:
+                    nc.vector.tensor_scalar(out=dst, in0=src, scalar1=OUT_SCALE, scalar2=None, op0=MULT)
                 else:
-                    nc.vector.tensor_copy(out=dst, in_=src)
-            x_tiles[k] = xg
-
-        def quantize_x(k):
-            xg = x_tiles[k]
-            xc = xs.tile([P, XCOLS * NB], U32, name="xc", align_bytes=64)
-            xsc = xs.tile([P, XCOLS * NB], U8, name="xsc", align_bytes=64)
-            flat = xg[:].rearrange("p c b t -> p (c b t)")
-            for w0, wn in ((0, 512), (512, 64)):
-                nc.vector.quantize_mx(
-                    out=xc[:, w0:w0 + wn].bitcast(FP8X4),
-                    scales=xsc[:, w0:w0 + wn],
-                    in_=flat[:, PACK * w0:PACK * (w0 + wn)],
-                )
-            x_tiles[k] = (xc, xsc)
-
-        nc.sync.dma_start(out=scale_sb[:], in_=psi_scale.rearrange("o (p t) z -> p (o t z)", t=PACK))
-        for j in range(4):
-            load_psi(j)
-        for j in range(N_TILES):
-            cast(j)
-            if j + 4 < N_TILES:
-                load_psi(j + 4)
-            if j == 3:
-                for h in range(4):
-                    nc.sync.dma_start(out=x_raw[:, 16 * h:16 * (h + 1)], in_=x_view[:, 16 * h:16 * (h + 1)])
-            if j >= 1:
-                scale_and_permute(j - 1)
-        permute_x(0, "scalar")
-        permute_x(1, "scalar")
-        scale_and_permute(N_TILES - 1)
-        quantize_x(0)
-        quantize_psi(7)
-        quantize_psi(6)
-        quantize_x(1)
-        late_quantize = [5, 4, 3, 2, 1, 0]
-
-        rs = [big.tile([P, R_OFFSETS[-1]], F32, name="r0", align_bytes=64, offset=OFF_R0),
-              big.tile([P, R_OFFSETS[-1]], F32, name="r1", align_bytes=64, offset=OFF_RAW)]
-        fs = [big.tile([P, NB, OUTW], F32, name="f%d" % i, align_bytes=64, offset=PARTS[i][2]) for i in range(3)]
-
-        def rblock(k, bi):
-            return rs[k % 2][:, R_OFFSETS[bi]:R_OFFSETS[bi + 1]].rearrange("p (b u m) -> p b u m", b=NB, m=BLOCKS[bi][3])
-
-        def compact(k, bi):
-            for l, r0 in BLOCKS[bi][5]:
-                d = 2 * l + 1
-                cl = OUT_OFFSETS[l]
-                nc.vector.tensor_copy(
-                    out=fs[(2 - k) % 3][:, :, cl:cl + d * d].rearrange("p b (u m) -> p b u m", m=d),
-                    in_=rblock(k, bi)[:, :, r0:r0 + d, r0:r0 + d],
-                )
-
-        def store(k):
-            nc.sync.dma_start(out=out[:, k * NB:(k + 1) * NB, :], in_=fs[(2 - k) % 3][:])
-
-        for k in range(N_CHUNKS):
-            xc, xsc = x_tiles[k]
-            bank = 0
-            for bi, (win, row0, rows, pitch, quads, degrees) in enumerate(BLOCKS):
-                for j, (stat, lo, hi) in enumerate(quads):
-                    pt = psum.tile([P, 4, WIN * NB], F32, name="pt")
-                    for mi, c in enumerate(stat):
-                        nc.tensor.matmul_mx(
-                            out=pt[:, mi, :],
-                            lhsT=psi_codes[:, c, :].bitcast(FP8X4),
-                            lhsT_scale=psi_scl[:, c, :],
-                            rhs=xc[:, win * NB:(win + WIN) * NB].bitcast(FP8X4),
-                            rhs_scale=xsc[:, win * NB:(win + WIN) * NB],
-                            start=True,
-                            stop=True,
-                        )
-                    src = pt[:, :, lo * NB:hi * NB].rearrange("p m (u b) -> p b u m", b=NB)
-                    dst = rblock(k, bi)[:, :, lo - row0:hi - row0, 4 * j:4 * j + 4]
-                    if bank in VECTOR_BANKS and k > 0:
-                        nc.vector.tensor_scalar(out=dst, in0=src, scalar1=OUT_SCALE, scalar2=None, op0=MULT)
-                    else:
-                        nc.scalar.activation(out=dst, in_=src, func=COPY, scale=OUT_SCALE)
-                    bank += 1
-                if k == 0:
-                    for q in late_quantize[:(2, 1, 1, 2, 0)[bi]]:
-                        quantize_psi(q)
-                    late_quantize = late_quantize[(2, 1, 1, 2, 0)[bi]:]
-                if bi == 0:
-                    if k > 0:
-                        compact(k - 1, len(BLOCKS) - 1)
-                        store(k - 1)
-                    if k + 2 < N_CHUNKS:
-                        permute_x(k + 2, "vector")
-                else:
-                    compact(k, bi - 1)
-                    if bi == 1 and k + 2 < N_CHUNKS:
-                        quantize_x(k + 2)
-        compact(N_CHUNKS - 1, len(BLOCKS) - 1)
-        store(N_CHUNKS - 1)
+                    nc.scalar.activation(out=dst, in_=src, func=COPY, scale=OUT_SCALE)
+            if grp in (0, 1, 4):
+                nc.sync.dma_start(out=out[:, HB * h:HB * (h + 1), 4 * line0:4 * (line0 + lines)], in_=ot[:])

@@ -23,11 +23,14 @@ N_TILES = G // GT
 QC = 16
 OUT_SCALE = 1.0 / (F ** 0.5)
 
-GROUPS = ((114, 169, 48), (72, 113, 36), (42, 71, 25), (21, 41, 16), (0, 20, 0))
-PIECES = ((114, 56), (72, 42), (0, 72))
-GROUP_PIECE = (0, 1, 2, 2, 2)
-STAGES = ((0, 0), (0, 1), (1, 0), (1, 1), (2, 0), (3, 0), (4, 0), (2, 1), (3, 1), (4, 1))
-VECTOR_FROM_STAGE = 7
+GROUPS = ((114, 169, 48), (72, 113, 36), (42, 71, 25), (32, 41, 16), (21, 31, 16), (0, 20, 0))
+X_TILE_OF_GROUP = (0, 1, 2, 3, 3, 4)
+X_BASES = (48, 36, 25, 16, 0)
+assert all(GROUPS[g][2] == X_BASES[X_TILE_OF_GROUP[g]] for g in range(len(GROUPS)))
+PIECES = ((114, 56), (72, 42), (32, 40), (0, 32))
+GROUP_PIECE = (0, 1, 2, 2, 3, 3)
+STAGES = (((0,), 0, 0), ((0,), 1, 0), ((1,), 0, 1), ((1,), 1, 1), ((2, 3), 0, 2), ((2, 3), 1, 2), ((4, 5), 0, 3), ((4, 5), 1, 3))
+VECTOR_SHARES = (6, 7)
 
 
 def make_words():
@@ -68,16 +71,15 @@ def make_jobs(first, last, base):
 
 JOBS = [make_jobs(first, last, base) for first, last, base in GROUPS]
 
-O7_BYTES = PIECES[0][1] * 4 * HB * 4
-O6_BYTES = PIECES[1][1] * 4 * HB * 4
-OB_BYTES = PIECES[2][1] * 4 * HB * 4
+SLOT_BYTES = PIECES[0][1] * 4 * HB * 4
+LOW_BYTES = PIECES[3][1] * 4 * HB * 4
 RAW_BYTES = GT * PACK * S2
 W_BYTES = G * PACK * S2 * 2
 GROUPED_BYTES = QC * G * PACK * 2
-OFF_W = 2 * O7_BYTES
+OFF_W = 2 * SLOT_BYTES
 OFF_GROUPED = OFF_W + W_BYTES
-PIECE_OFFSETS = ((0, O7_BYTES), (0, O7_BYTES), (OFF_W, OFF_W + OB_BYTES))
-assert N_TILES * RAW_BYTES <= 2 * O7_BYTES and O6_BYTES <= O7_BYTES and 2 * OB_BYTES <= W_BYTES + GROUPED_BYTES
+PIECE_OFFSETS = ((0, SLOT_BYTES), (0, SLOT_BYTES), (0, SLOT_BYTES), (OFF_W, OFF_W + LOW_BYTES))
+assert N_TILES * RAW_BYTES <= 2 * SLOT_BYTES and 2 * LOW_BYTES <= W_BYTES
 
 
 def tile_s2conv_pa_kernel(tc, x, psi_bytes, psi_scale, out):
@@ -86,7 +88,7 @@ def tile_s2conv_pa_kernel(tc, x, psi_bytes, psi_scale, out):
         keep = ctx.enter_context(tc.tile_pool(name="keep", bufs=1))
         big = ctx.enter_context(tc.tile_pool(name="big", bufs=1))
         xgs = ctx.enter_context(tc.tile_pool(name="xgs", bufs=2))
-        xcs = ctx.enter_context(tc.tile_pool(name="xcs", bufs=4))
+        xcs = ctx.enter_context(tc.tile_pool(name="xcs", bufs=5))
         psum = ctx.enter_context(tc.psum_pool(name="psum", bufs=8))
         ctx.enter_context(tc.manual_schedule())
 
@@ -102,9 +104,10 @@ def tile_s2conv_pa_kernel(tc, x, psi_bytes, psi_scale, out):
         psi_view = psi_bytes.rearrange("g (p t) c -> p g t c", t=PACK)
         x_view = x.rearrange("b (p t) c -> p b t c", t=PACK)
 
-        nc.sync.dma_start(out=scale_sb[:], in_=psi_scale.rearrange("o (p t) z -> p (o t z)", t=PACK))
         for j in range(N_TILES):
             nc.sync.dma_start(out=raws[j][:], in_=psi_view[:, j * GT:(j + 1) * GT])
+            if j == 1:
+                nc.sync.dma_start(out=scale_sb[:], in_=psi_scale.rearrange("o (p t) z -> p (o t z)", t=PACK))
         for h in range(2):
             for e in range(2):
                 nc.sync.dma_start(out=x_raw[h][:, 16 * e:16 * (e + 1)], in_=x_view[:, HB * h + 16 * e:HB * h + 16 * (e + 1)])
@@ -140,7 +143,7 @@ def tile_s2conv_pa_kernel(tc, x, psi_bytes, psi_scale, out):
         x_ready = {}
 
         def permute_x(grp, h, engine):
-            base = GROUPS[grp][2]
+            base = X_BASES[grp]
             xg = xgs.tile([P, 16, HB, PACK], BF16, name="xg", align_bytes=64)
             dst = xg[:].rearrange("p (r j) b t -> p j b t r", r=4)
             src = x_raw[h][:, :, :, base:base + 16].rearrange("p b t (j r) -> p j b t r", r=4)
@@ -166,11 +169,9 @@ def tile_s2conv_pa_kernel(tc, x, psi_bytes, psi_scale, out):
             scale_quarter(3, 2 * GT * pair, 2 * GT * (pair + 1))
             permute_quarter(3, 0, QC, 2 * GT * pair, 2 * GT * (pair + 1))
         permute_x(0, 0, "scalar")
-        permute_x(0, 1, "scalar")
         quantize_x(0, 0)
         quantize_quarter(3, 0)
         quantize_quarter(3, 1)
-        quantize_x(0, 1)
 
         later = []
 
@@ -181,19 +182,25 @@ def tile_s2conv_pa_kernel(tc, x, psi_bytes, psi_scale, out):
             later.append((None, lambda: quantize_quarter(q, 0)))
             later.append((("quarter", q), lambda: quantize_quarter(q, 1)))
 
-        def add_x_pair(a, b):
-            later.append((None, lambda: permute_x(a[0], a[1], "vector")))
-            later.append((None, lambda: permute_x(b[0], b[1], "vector")))
+        def add_x_pair(a, b, engine):
+            later.append((None, lambda: permute_x(a[0], a[1], engine)))
+            later.append((None, lambda: permute_x(b[0], b[1], engine)))
             later.append((("x", a), lambda: quantize_x(a[0], a[1])))
             later.append((("x", b), lambda: quantize_x(b[0], b[1])))
 
-        add_quarter(2)
-        add_x_pair((1, 0), (1, 1))
+        later.append((None, lambda: scale_quarter(2, 0, G)))
+        later.append((None, lambda: permute_quarter(2, 0, 8, 0, G)))
+        later.append((None, lambda: permute_x(0, 1, "vector")))
+        later.append((None, lambda: permute_quarter(2, 8, QC, 0, G)))
+        later.append((("x", (0, 1)), lambda: quantize_x(0, 1)))
+        later.append((None, lambda: quantize_quarter(2, 0)))
+        later.append((("quarter", 2), lambda: quantize_quarter(2, 1)))
+        add_x_pair((1, 0), (1, 1), "vector")
         add_quarter(1)
-        add_x_pair((2, 0), (3, 0))
+        add_x_pair((2, 0), (3, 0), "vector")
+        add_x_pair((2, 1), (3, 1), "vector")
         add_quarter(0)
-        add_x_pair((4, 0), (2, 1))
-        add_x_pair((3, 1), (4, 1))
+        add_x_pair((4, 0), (4, 1), "vector")
         done = set()
 
         def need(what):
@@ -202,40 +209,42 @@ def tile_s2conv_pa_kernel(tc, x, psi_bytes, psi_scale, out):
                 call()
                 done.add((len(done), key) if key is None else key)
 
-        NEEDS = {2: (("quarter", 2), ("x", (1, 0))), 3: (("x", (1, 1)),), 4: (("quarter", 1), ("x", (2, 0)), ("permuted", 0)),
-                 5: (("x", (3, 0)),), 6: (("quarter", 0), ("x", (4, 0))), 7: (("x", (2, 1)),), 8: (("x", (3, 1)),), 9: (("x", (4, 1)),)}
+        NEEDS = {1: (("x", (0, 1)),), 2: (("quarter", 2), ("x", (1, 0))), 3: (("x", (1, 1)),), 4: (("quarter", 1), ("x", (3, 0))),
+                 5: (("x", (3, 1)),), 6: (("quarter", 0), ("x", (4, 1)))}
 
         out_tiles = {}
-        for k, (grp, h) in enumerate(STAGES):
+        for k, (groups, h, finished) in enumerate(STAGES):
             for what in NEEDS.get(k, ()):
                 need(what)
-            if k == VECTOR_FROM_STAGE:
-                need(("x", (4, 1)))
-            piece = GROUP_PIECE[grp]
-            line0, lines = PIECES[piece]
-            if (piece, h) not in out_tiles:
-                out_tiles[(piece, h)] = big.tile([P, HB, 4 * lines], F32, name="o%d%d" % (piece, h), align_bytes=64,
-                                                 offset=PIECE_OFFSETS[piece][h])
-            ot = out_tiles[(piece, h)]
-            xc, xsc = x_ready[(grp, h)]
-            for n, (line, step, count, first_slot, passes) in enumerate(JOBS[grp]):
-                pt = psum.tile([P, 512], F32, name="pt")
-                for f, (c, r, shift) in enumerate(passes):
-                    nc.tensor.matmul_mx(
-                        out=pt[:, 128 * f - HB * shift:128 * (f + 1) - HB * shift],
-                        lhsT=psi_codes[:, c, :].bitcast(FP8X4),
-                        lhsT_scale=psi_scl[:, c, :],
-                        rhs=xc[:, 128 * r:128 * (r + 1)].bitcast(FP8X4),
-                        rhs_scale=xsc[:, 128 * r:128 * (r + 1)],
-                        start=True,
-                        stop=True,
-                    )
-                src = pt[:].rearrange("p (f j b) -> p b j f", f=4, j=4)[:, :, first_slot:first_slot + count, :]
-                n0 = line - line0
-                dst = ot[:].rearrange("p b (n f) -> p b n f", f=4)[:, :, n0:n0 + step * (count - 1) + 1:step, :]
-                if k >= VECTOR_FROM_STAGE and n % 2 == 1:
-                    nc.vector.tensor_scalar(out=dst, in0=src, scalar1=OUT_SCALE, scalar2=None, op0=MULT)
-                else:
-                    nc.scalar.activation(out=dst, in_=src, func=COPY, scale=OUT_SCALE)
-            if grp in (0, 1, 4):
-                nc.sync.dma_start(out=out[:, HB * h:HB * (h + 1), 4 * line0:4 * (line0 + lines)], in_=ot[:])
+            n = 0
+            for grp in groups:
+                piece = GROUP_PIECE[grp]
+                line0, lines = PIECES[piece]
+                if (piece, h) not in out_tiles:
+                    out_tiles[(piece, h)] = big.tile([P, HB, 4 * lines], F32, name="o%d%d" % (piece, h), align_bytes=64,
+                                                     offset=PIECE_OFFSETS[piece][h])
+                ot = out_tiles[(piece, h)]
+                xc, xsc = x_ready[(X_TILE_OF_GROUP[grp], h)]
+                for line, step, count, first_slot, passes in JOBS[grp]:
+                    pt = psum.tile([P, 512], F32, name="pt")
+                    for f, (c, r, shift) in enumerate(passes):
+                        nc.tensor.matmul_mx(
+                            out=pt[:, 128 * f - HB * shift:128 * (f + 1) - HB * shift],
+                            lhsT=psi_codes[:, c, :].bitcast(FP8X4),
+                            lhsT_scale=psi_scl[:, c, :],
+                            rhs=xc[:, 128 * r:128 * (r + 1)].bitcast(FP8X4),
+                            rhs_scale=xsc[:, 128 * r:128 * (r + 1)],
+                            start=True,
+                            stop=True,
+                        )
+                    src = pt[:].rearrange("p (f j b) -> p b j f", f=4, j=4)[:, :, first_slot:first_slot + count, :]
+                    n0 = line - line0
+                    dst = ot[:].rearrange("p b (n f) -> p b n f", f=4)[:, :, n0:n0 + step * (count - 1) + 1:step, :]
+                    if k in VECTOR_SHARES and n % 2 == 1:
+                        nc.vector.tensor_scalar(out=dst, in0=src, scalar1=OUT_SCALE, scalar2=None, op0=MULT)
+                    else:
+                        nc.scalar.activation(out=dst, in_=src, func=COPY, scale=OUT_SCALE)
+                    n += 1
+            if finished is not None:
+                line0, lines = PIECES[finished]
+                nc.sync.dma_start(out=out[:, HB * h:HB * (h + 1), 4 * line0:4 * (line0 + lines)], in_=out_tiles[(finished, h)][:])

@@ -29,8 +29,9 @@ X_BASES = (48, 36, 25, 16, 0)
 assert all(GROUPS[g][2] == X_BASES[X_TILE_OF_GROUP[g]] for g in range(len(GROUPS)))
 PIECES = ((114, 56), (72, 42), (32, 40), (0, 32))
 GROUP_PIECE = (0, 1, 2, 2, 3, 3)
-STAGES = (((0,), 0, 0), ((0,), 1, 0), ((1,), 0, 1), ((1,), 1, 1), ((2, 3), 0, 2), ((2, 3), 1, 2), ((4, 5), 0, 3), ((4, 5), 1, 3))
-VECTOR_SHARES = (6, 7)
+STAGES = (((0,), 0, 0), ((0,), 1, 0), ((1,), 0, 1), ((1,), 1, 1), ((2, 3), 0, 2), ((2, 3), 1, 2), ((4,), 0, None), ((4,), 1, None),
+          ((5,), 0, 3), ((5,), 1, 3))
+VECTOR_SHARES = (8, 9)
 
 
 def make_words():
@@ -76,10 +77,13 @@ LOW_BYTES = PIECES[3][1] * 4 * HB * 4
 RAW_BYTES = GT * PACK * S2
 W_BYTES = G * PACK * S2 * 2
 GROUPED_BYTES = QC * G * PACK * 2
-OFF_W = 2 * SLOT_BYTES
+THIRD_BYTES = PIECES[1][1] * 4 * HB * 4
+OFF_THIRD = 2 * SLOT_BYTES
+OFF_W = OFF_THIRD + THIRD_BYTES
 OFF_GROUPED = OFF_W + W_BYTES
-PIECE_OFFSETS = ((0, SLOT_BYTES), (0, SLOT_BYTES), (0, SLOT_BYTES), (OFF_W, OFF_W + LOW_BYTES))
-assert N_TILES * RAW_BYTES <= 2 * SLOT_BYTES and 2 * LOW_BYTES <= W_BYTES
+PIECE_OFFSETS = ((0, SLOT_BYTES), (OFF_THIRD, 0), (SLOT_BYTES, OFF_THIRD), (OFF_W, OFF_W + LOW_BYTES))
+assert N_TILES * RAW_BYTES <= 2 * SLOT_BYTES and 2 * LOW_BYTES <= W_BYTES and GROUPED_BYTES <= THIRD_BYTES
+assert PIECES[2][1] <= PIECES[1][1]
 
 
 def tile_s2conv_pa_kernel(tc, x, psi_bytes, psi_scale, out):
@@ -88,7 +92,7 @@ def tile_s2conv_pa_kernel(tc, x, psi_bytes, psi_scale, out):
         keep = ctx.enter_context(tc.tile_pool(name="keep", bufs=1))
         big = ctx.enter_context(tc.tile_pool(name="big", bufs=1))
         xgs = ctx.enter_context(tc.tile_pool(name="xgs", bufs=2))
-        xcs = ctx.enter_context(tc.tile_pool(name="xcs", bufs=5))
+        xcs = ctx.enter_context(tc.tile_pool(name="xcs", bufs=4))
         psum = ctx.enter_context(tc.psum_pool(name="psum", bufs=8))
         ctx.enter_context(tc.manual_schedule())
 
@@ -99,7 +103,8 @@ def tile_s2conv_pa_kernel(tc, x, psi_bytes, psi_scale, out):
 
         raws = [big.tile([P, GT, PACK, S2], U8, name="raw%d" % j, align_bytes=64, offset=j * RAW_BYTES) for j in range(N_TILES)]
         w = big.tile([P, G, PACK, S2], BF16, name="w", align_bytes=64, offset=OFF_W)
-        grouped = big.tile([P, QC, G, PACK], BF16, name="grouped", align_bytes=64, offset=OFF_GROUPED)
+        grouped_first = big.tile([P, QC, G, PACK], BF16, name="grouped_first", align_bytes=64, offset=OFF_THIRD)
+        grouped_half = big.tile([P, QC // 2, G, PACK], BF16, name="grouped_half", align_bytes=64, offset=OFF_GROUPED)
 
         psi_view = psi_bytes.rearrange("g (p t) c -> p g t c", t=PACK)
         x_view = x.rearrange("b (p t) c -> p b t c", t=PACK)
@@ -125,18 +130,17 @@ def tile_s2conv_pa_kernel(tc, x, psi_bytes, psi_scale, out):
                 part = w[:, g0:g1, t, QC * q:QC * (q + 1)]
                 nc.vector.tensor_scalar(out=part, in0=part, scalar1=scale_sb[:, t:t + 1], scalar2=None, op0=MULT)
 
-        def permute_quarter(q, c0, c1, g0, g1):
+        def permute_columns(dst, c0, n, g0, g1):
             nc.vector.tensor_copy(
-                out=grouped[:, c0:c1, g0:g1, :].rearrange("p (cb i) g t -> p cb g t i", i=4),
-                in_=w[:, g0:g1, :, QC * q + c0:QC * q + c1].rearrange("p g t (cb i) -> p cb g t i", i=4),
+                out=dst[:, :, g0:g1, :].rearrange("p (cb i) g t -> p cb g t i", i=4),
+                in_=w[:, g0:g1, :, c0:c0 + n].rearrange("p g t (cb i) -> p cb g t i", i=4),
             )
 
-        def quantize_quarter(q, e):
-            c0 = QC * q + 8 * e
+        def quantize_columns(src, c0):
             nc.vector.quantize_mx(
                 out=psi_codes[:, c0:c0 + 8, :].rearrange("p c g -> p (c g)").bitcast(FP8X4),
                 scales=psi_scl[:, c0:c0 + 8, :].rearrange("p c g -> p (c g)"),
-                in_=grouped[:, 8 * e:8 * (e + 1)].rearrange("p c g t -> p (c g t)"),
+                in_=src.rearrange("p c g t -> p (c g t)"),
             )
 
         x_grouped = {}
@@ -167,20 +171,26 @@ def tile_s2conv_pa_kernel(tc, x, psi_bytes, psi_scale, out):
             cast(2 * pair, "scalar")
             cast(2 * pair + 1, "vector")
             scale_quarter(3, 2 * GT * pair, 2 * GT * (pair + 1))
-            permute_quarter(3, 0, QC, 2 * GT * pair, 2 * GT * (pair + 1))
+            permute_columns(grouped_first, 3 * QC, QC, 2 * GT * pair, 2 * GT * (pair + 1))
         permute_x(0, 0, "scalar")
+        permute_x(0, 1, "scalar")
         quantize_x(0, 0)
-        quantize_quarter(3, 0)
-        quantize_quarter(3, 1)
+        quantize_columns(grouped_first[:, 0:8], 3 * QC)
+        quantize_columns(grouped_first[:, 8:QC], 3 * QC + 8)
+        quantize_x(0, 1)
 
         later = []
 
-        def add_quarter(q):
+        def add_quarter(q, a, b):
             later.append((None, lambda: scale_quarter(q, 0, G)))
-            later.append((None, lambda: permute_quarter(q, 0, 8, 0, G)))
-            later.append((("permuted", q), lambda: permute_quarter(q, 8, QC, 0, G)))
-            later.append((None, lambda: quantize_quarter(q, 0)))
-            later.append((("quarter", q), lambda: quantize_quarter(q, 1)))
+            later.append((None, lambda: permute_columns(grouped_half, QC * q, 8, 0, G)))
+            later.append((None, lambda: permute_x(a[0], a[1], "vector")))
+            later.append((None, lambda: quantize_columns(grouped_half[:], QC * q)))
+            later.append((("permuted", q), lambda: permute_columns(grouped_half, QC * q + 8, 8, 0, G)))
+            later.append((None, lambda: permute_x(b[0], b[1], "vector")))
+            later.append((("quarter", q), lambda: quantize_columns(grouped_half[:], QC * q + 8)))
+            later.append((("x", a), lambda: quantize_x(a[0], a[1])))
+            later.append((("x", b), lambda: quantize_x(b[0], b[1])))
 
         def add_x_pair(a, b, engine):
             later.append((None, lambda: permute_x(a[0], a[1], engine)))
@@ -188,19 +198,10 @@ def tile_s2conv_pa_kernel(tc, x, psi_bytes, psi_scale, out):
             later.append((("x", a), lambda: quantize_x(a[0], a[1])))
             later.append((("x", b), lambda: quantize_x(b[0], b[1])))
 
-        later.append((None, lambda: scale_quarter(2, 0, G)))
-        later.append((None, lambda: permute_quarter(2, 0, 8, 0, G)))
-        later.append((None, lambda: permute_x(0, 1, "vector")))
-        later.append((None, lambda: permute_quarter(2, 8, QC, 0, G)))
-        later.append((("x", (0, 1)), lambda: quantize_x(0, 1)))
-        later.append((None, lambda: quantize_quarter(2, 0)))
-        later.append((("quarter", 2), lambda: quantize_quarter(2, 1)))
-        add_x_pair((1, 0), (1, 1), "vector")
-        add_quarter(1)
-        add_x_pair((2, 0), (3, 0), "vector")
+        add_quarter(2, (1, 0), (1, 1))
+        add_quarter(1, (2, 0), (3, 0))
         add_x_pair((2, 1), (3, 1), "vector")
-        add_quarter(0)
-        add_x_pair((4, 0), (4, 1), "vector")
+        add_quarter(0, (4, 0), (4, 1))
         done = set()
 
         def need(what):
@@ -209,8 +210,8 @@ def tile_s2conv_pa_kernel(tc, x, psi_bytes, psi_scale, out):
                 call()
                 done.add((len(done), key) if key is None else key)
 
-        NEEDS = {1: (("x", (0, 1)),), 2: (("quarter", 2), ("x", (1, 0))), 3: (("x", (1, 1)),), 4: (("quarter", 1), ("x", (3, 0))),
-                 5: (("x", (3, 1)),), 6: (("quarter", 0), ("x", (4, 1)))}
+        NEEDS = {2: (("quarter", 2), ("x", (1, 0))), 3: (("x", (1, 1)),), 4: (("quarter", 1), ("x", (3, 0))),
+                 5: (("x", (3, 1)),), 6: (("permuted", 0),), 8: (("quarter", 0), ("x", (4, 1)))}
 
         out_tiles = {}
         for k, (groups, h, finished) in enumerate(STAGES):

@@ -31,7 +31,7 @@ PIECES = ((114, 56), (72, 42), (32, 40), (0, 32))
 GROUP_PIECE = (0, 1, 2, 2, 3, 3)
 STAGES = (((0,), 0, 0), ((0,), 1, 0), ((1,), 0, 1), ((1,), 1, 1), ((2, 3), 0, 2), ((2, 3), 1, 2), ((4,), 0, None), ((4,), 1, None),
           ((5,), 0, 3), ((5,), 1, 3))
-VECTOR_SHARES = (8, 9)
+VECTOR_SHARES = (0, 8, 9)
 
 
 def make_words():

@@ -18,7 +18,7 @@ MULT = mybir.AluOpType.mult
 P = 128
 PACK = 4
 HB = 32
-GT = 16
+GT = 8
 N_TILES = G // GT
 QC = 16
 OUT_SCALE = 1.0 / (F ** 0.5)
@@ -111,7 +111,7 @@ def tile_s2conv_pa_kernel(tc, x, psi_bytes, psi_scale, out):
 
         for j in range(N_TILES):
             nc.sync.dma_start(out=raws[j][:], in_=psi_view[:, j * GT:(j + 1) * GT])
-            if j == 1:
+            if j == 3:
                 nc.sync.dma_start(out=scale_sb[:], in_=psi_scale.rearrange("o (p t) z -> p (o t z)", t=PACK))
         for h in range(2):
             for e in range(2):
@@ -174,10 +174,9 @@ def tile_s2conv_pa_kernel(tc, x, psi_bytes, psi_scale, out):
             permute_columns(grouped_first, 3 * QC, QC, 2 * GT * pair, 2 * GT * (pair + 1))
         permute_x(0, 0, "scalar")
         permute_x(0, 1, "scalar")
-        quantize_x(0, 0)
         quantize_columns(grouped_first[:, 0:8], 3 * QC)
         quantize_columns(grouped_first[:, 8:QC], 3 * QC + 8)
-        quantize_x(0, 1)
+        quantize_x(0, 0)
 
         later = []
 
@@ -198,6 +197,7 @@ def tile_s2conv_pa_kernel(tc, x, psi_bytes, psi_scale, out):
             later.append((("x", a), lambda: quantize_x(a[0], a[1])))
             later.append((("x", b), lambda: quantize_x(b[0], b[1])))
 
+        later.append((("x", (0, 1)), lambda: quantize_x(0, 1)))
         add_quarter(2, (1, 0), (1, 1))
         add_quarter(1, (2, 0), (3, 0))
         add_x_pair((2, 1), (3, 1), "vector")
@@ -210,7 +210,7 @@ def tile_s2conv_pa_kernel(tc, x, psi_bytes, psi_scale, out):
                 call()
                 done.add((len(done), key) if key is None else key)
 
-        NEEDS = {2: (("quarter", 2), ("x", (1, 0))), 3: (("x", (1, 1)),), 4: (("quarter", 1), ("x", (3, 0))),
+        NEEDS = {1: (("x", (0, 1)),), 2: (("quarter", 2), ("x", (1, 0))), 3: (("x", (1, 1)),), 4: (("quarter", 1), ("x", (3, 0))),
                  5: (("x", (3, 1)),), 6: (("permuted", 0),), 8: (("quarter", 0), ("x", (4, 1)))}
 
         out_tiles = {}
@@ -241,7 +241,7 @@ def tile_s2conv_pa_kernel(tc, x, psi_bytes, psi_scale, out):
                     src = pt[:].rearrange("p (f j b) -> p b j f", f=4, j=4)[:, :, first_slot:first_slot + count, :]
                     n0 = line - line0
                     dst = ot[:].rearrange("p b (n f) -> p b n f", f=4)[:, :, n0:n0 + step * (count - 1) + 1:step, :]
-                    if k in VECTOR_SHARES and n % 2 == 1:
+                    if k in VECTOR_SHARES and (n % 2 == 1 or (k == 0 and n == 0)):
                         nc.vector.tensor_scalar(out=dst, in0=src, scalar1=OUT_SCALE, scalar2=None, op0=MULT)
                     else:
                         nc.scalar.activation(out=dst, in_=src, func=COPY, scale=OUT_SCALE)

@@ -18,7 +18,7 @@ MULT = mybir.AluOpType.mult
 P = 128
 PACK = 4
 HB = 32
-GT = 8
+GT = 16
 N_TILES = G // GT
 QC = 16
 OUT_SCALE = 1.0 / (F ** 0.5)
@@ -32,6 +32,7 @@ GROUP_PIECE = (0, 1, 2, 2, 3, 3)
 STAGES = (((0,), 0, 0), ((0,), 1, 0), ((1,), 0, 1), ((1,), 1, 1), ((2, 3), 0, 2), ((2, 3), 1, 2), ((4,), 0, None), ((4,), 1, None),
           ((5,), 0, 3), ((5,), 1, 3))
 VECTOR_SHARES = (0, 8, 9)
+WARM_PASSES = 8
 
 
 def make_words():
@@ -111,7 +112,7 @@ def tile_s2conv_pa_kernel(tc, x, psi_bytes, psi_scale, out):
 
         for j in range(N_TILES):
             nc.sync.dma_start(out=raws[j][:], in_=psi_view[:, j * GT:(j + 1) * GT])
-            if j == 3:
+            if j == 1:
                 nc.sync.dma_start(out=scale_sb[:], in_=psi_scale.rearrange("o (p t) z -> p (o t z)", t=PACK))
         for h in range(2):
             for e in range(2):
@@ -172,6 +173,10 @@ def tile_s2conv_pa_kernel(tc, x, psi_bytes, psi_scale, out):
             cast(2 * pair + 1, "vector")
             scale_quarter(3, 2 * GT * pair, 2 * GT * (pair + 1))
             permute_columns(grouped_first, 3 * QC, QC, 2 * GT * pair, 2 * GT * (pair + 1))
+        warm = psum.tile([P, 512], F32, name="pt")
+        for i in range(WARM_PASSES):
+            nc.tensor.matmul(out=warm[:], lhsT=grouped_first[:, 0, 0:32, :].rearrange("p g t -> p (g t)"),
+                             rhs=grouped_first[:, 8 + i % 8, :, :].rearrange("p g t -> p (g t)"), start=True, stop=True)
         permute_x(0, 0, "scalar")
         permute_x(0, 1, "scalar")
         quantize_columns(grouped_first[:, 0:8], 3 * QC)

@@ -185,10 +185,10 @@ def tile_s2conv_pa_kernel(tc, x, psi_bytes, psi_scale, out):
 
         later = []
 
-        def add_quarter(q, a, b):
+        def add_quarter(q, a, b, engine_a="vector"):
             later.append((None, lambda: scale_quarter(q, 0, G)))
             later.append((None, lambda: permute_columns(grouped_half, QC * q, 8, 0, G)))
-            later.append((None, lambda: permute_x(a[0], a[1], "vector")))
+            later.append((None, lambda: permute_x(a[0], a[1], engine_a)))
             later.append((None, lambda: quantize_columns(grouped_half[:], QC * q)))
             later.append((("permuted", q), lambda: permute_columns(grouped_half, QC * q + 8, 8, 0, G)))
             later.append((None, lambda: permute_x(b[0], b[1], "vector")))
@@ -203,7 +203,7 @@ def tile_s2conv_pa_kernel(tc, x, psi_bytes, psi_scale, out):
             later.append((("x", b), lambda: quantize_x(b[0], b[1])))
 
         later.append((("x", (0, 1)), lambda: quantize_x(0, 1)))
-        add_quarter(2, (1, 0), (1, 1))
+        add_quarter(2, (1, 0), (1, 1), "scalar")
         add_quarter(1, (2, 0), (3, 0))
         add_x_pair((2, 1), (3, 1), "vector")
         add_quarter(0, (4, 0), (4, 1))

from contextlib import ExitStack

import concourse.mybir as mybir

B, F, G, S2, L = 64, 512, 128, 64, 7
OUTW = 680
FLOPS = 2 * F * G * B * OUTW

F32 = mybir.dt.float32
BF16 = mybir.dt.bfloat16
U32 = mybir.dt.uint32
U8 = mybir.dt.uint8
FP8 = mybir.dt.float8_e4m3fn
FP8X4 = mybir.dt.float8_e4m3fn_x4
COPY = mybir.ActivationFunctionType.Copy
MULT = mybir.AluOpType.mult

P = 128
PACK = 4
HB = 32
GT = 16
N_TILES = G // GT
QC = 16
OUT_SCALE = 1.0 / (F ** 0.5)

GROUPS = ((114, 169, 48), (72, 113, 36), (42, 71, 25), (32, 41, 16), (21, 31, 16), (0, 20, 0))
X_TILE_OF_GROUP = (0, 1, 2, 3, 3, 4)
X_BASES = (48, 36, 25, 16, 0)
assert all(GROUPS[g][2] == X_BASES[X_TILE_OF_GROUP[g]] for g in range(len(GROUPS)))
PIECES = ((114, 56), (72, 42), (32, 40), (0, 32))
GROUP_PIECE = (0, 1, 2, 2, 3, 3)
STAGES = (((0,), 0, 0), ((0,), 1, 0), ((1,), 0, 1), ((1,), 1, 1), ((2, 3), 0, 2), ((2, 3), 1, 2), ((4,), 0, None), ((4,), 1, None),
          ((5,), 0, 3), ((5,), 1, 3))
VECTOR_SHARES = (0, 8, 9)
WARM_PASSES = 8


def make_words():
    words = []
    for l in range(L + 1):
        d = 2 * l + 1
        for u in range(d):
            for m in range(d):
                words.append((l * l + m, l * l + u, d))
    return words


WORDS = make_words()


def make_jobs(first, last, base):
    jobs = []
    taken = set()
    for line in range(first, last + 1):
        if line in taken:
            continue
        quad = WORDS[4 * line:4 * line + 4]
        step = quad[0][2]
        count = 1
        while line + count * step <= last:
            later = WORDS[4 * (line + count * step):4 * (line + count * step) + 4]
            if all(a[0] == b[0] and b[1] == a[1] + 4 * count for a, b in zip(quad, later)):
                count += 1
            else:
                break
        for j in range(count):
            taken.add(line + j * step)
        first_slot = (quad[0][1] - base) // 4
        passes = tuple((q[0], (q[1] - base) % 4, (q[1] - base) // 4 - first_slot) for q in quad)
        jobs.append((line, step, count, first_slot, passes))
    return jobs


JOBS = [make_jobs(first, last, base) for first, last, base in GROUPS]

SLOT_BYTES = PIECES[0][1] * 4 * HB * 4
LOW_BYTES = PIECES[3][1] * 4 * HB * 4
RAW_BYTES = GT * PACK * S2
W_BYTES = G * PACK * S2 * 2
GROUPED_BYTES = QC * G * PACK * 2
THIRD_BYTES = PIECES[1][1] * 4 * HB * 4
OFF_THIRD = 2 * SLOT_BYTES
OFF_W = OFF_THIRD + THIRD_BYTES
OFF_GROUPED = OFF_W + W_BYTES
PIECE_OFFSETS = ((0, SLOT_BYTES), (OFF_THIRD, 0), (SLOT_BYTES, OFF_THIRD), (OFF_W, OFF_W + LOW_BYTES))
assert N_TILES * RAW_BYTES <= 2 * SLOT_BYTES and 2 * LOW_BYTES <= W_BYTES and GROUPED_BYTES <= THIRD_BYTES
assert PIECES[2][1] <= PIECES[1][1]


def tile_s2conv_pa_kernel(tc, x, psi_bytes, psi_scale, out):
    nc = tc.nc
    with ExitStack() as ctx:
        keep = ctx.enter_context(tc.tile_pool(name="keep", bufs=1))
        big = ctx.enter_context(tc.tile_pool(name="big", bufs=1))
        xgs = ctx.enter_context(tc.tile_pool(name="xgs", bufs=2))
        xcs = ctx.enter_context(tc.tile_pool(name="xcs", bufs=4))
        psum = ctx.enter_context(tc.psum_pool(name="psum", bufs=8))
        ctx.enter_context(tc.manual_schedule())

        scale_sb = keep.tile([P, PACK], F32, name="scale_sb")
        psi_codes = keep.tile([P, S2, G], U32, name="psi_codes", align_bytes=64)
        psi_scl = keep.tile([P, S2, G], U8, name="psi_scl", align_bytes=64)
        x_raw = [keep.tile([P, HB, PACK, S2], BF16, name="x_raw%d" % h) for h in range(2)]

        raws = [big.tile([P, GT, PACK, S2], U8, name="raw%d" % j, align_bytes=64, offset=j * RAW_BYTES) for j in range(N_TILES)]
        w = big.tile([P, G, PACK, S2], BF16, name="w", align_bytes=64, offset=OFF_W)
        grouped_first = big.tile([P, QC, G, PACK], BF16, name="grouped_first", align_bytes=64, offset=OFF_THIRD)
        grouped_half = big.tile([P, QC // 2, G, PACK], BF16, name="grouped_half", align_bytes=64, offset=OFF_GROUPED)

        psi_view = psi_bytes.rearrange("g (p t) c -> p g t c", t=PACK)
        x_view = x.rearrange("b (p t) c -> p b t c", t=PACK)

        for j in range(N_TILES):
            nc.sync.dma_start(out=raws[j][:], in_=psi_view[:, j * GT:(j + 1) * GT])
            if j == 1:
                nc.sync.dma_start(out=scale_sb[:], in_=psi_scale.rearrange("o (p t) z -> p (o t z)", t=PACK))
        for h in range(2):
            for e in range(2):
                nc.sync.dma_start(out=x_raw[h][:, 16 * e:16 * (e + 1)], in_=x_view[:, HB * h + 16 * e:HB * h + 16 * (e + 1)])

        def cast(j, engine):
            src = raws[j][:].rearrange("p g t c -> p (g t c)").bitcast(FP8)
            dst = w[:, j * GT:(j + 1) * GT].rearrange("p g t c -> p (g t c)")
            if engine == "scalar":
                nc.scalar.copy(out=dst, in_=src)
            else:
                nc.vector.tensor_copy(out=dst, in_=src)

        def scale_quarter(q, g0, g1):
            for t in range(PACK):
                part = w[:, g0:g1, t, QC * q:QC * (q + 1)]
                nc.vector.tensor_scalar(out=part, in0=part, scalar1=scale_sb[:, t:t + 1], scalar2=None, op0=MULT)

        def permute_columns(dst, c0, n, g0, g1):
            nc.vector.tensor_copy(
                out=dst[:, :, g0:g1, :].rearrange("p (cb i) g t -> p cb g t i", i=4),
                in_=w[:, g0:g1, :, c0:c0 + n].rearrange("p g t (cb i) -> p cb g t i", i=4),
            )

        def quantize_columns(src, c0):
            nc.vector.quantize_mx(
                out=psi_codes[:, c0:c0 + 8, :].rearrange("p c g -> p (c g)").bitcast(FP8X4),
                scales=psi_scl[:, c0:c0 + 8, :].rearrange("p c g -> p (c g)"),
                in_=src.rearrange("p c g t -> p (c g t)"),
            )

        x_grouped = {}
        x_ready = {}

        def permute_x(grp, h, engine):
            base = X_BASES[grp]
            xg = xgs.tile([P, 16, HB, PACK], BF16, name="xg", align_bytes=64)
            dst = xg[:].rearrange("p (r j) b t -> p j b t r", r=4)
            src = x_raw[h][:, :, :, base:base + 16].rearrange("p b t (j r) -> p j b t r", r=4)
            if engine == "scalar":
                nc.scalar.copy(out=dst, in_=src)
            else:
                nc.vector.tensor_copy(out=dst, in_=src)
            x_grouped[(grp, h)] = xg

        def quantize_x(grp, h):
            xc = xcs.tile([P, 16 * HB], U32, name="xc", align_bytes=64)
            xsc = xcs.tile([P, 16 * HB], U8, name="xsc", align_bytes=64)
            nc.vector.quantize_mx(
                out=xc[:].bitcast(FP8X4),
                scales=xsc[:],
                in_=x_grouped[(grp, h)][:].rearrange("p s b t -> p (s b t)"),
            )
            x_ready[(grp, h)] = (xc, xsc)

        for pair in range(N_TILES // 2):
            cast(2 * pair, "scalar")
            cast(2 * pair + 1, "vector")
            scale_quarter(3, 2 * GT * pair, 2 * GT * (pair + 1))
            permute_columns(grouped_first, 3 * QC, QC, 2 * GT * pair, 2 * GT * (pair + 1))
        warm = psum.tile([P, 512], F32, name="pt")
        for i in range(WARM_PASSES):
            nc.tensor.matmul(out=warm[:], lhsT=grouped_first[:, 0, 0:32, :].rearrange("p g t -> p (g t)"),
                             rhs=grouped_first[:, 8 + i % 8, :, :].rearrange("p g t -> p (g t)"), start=True, stop=True)
        permute_x(0, 0, "scalar")
        permute_x(0, 1, "scalar")
        quantize_columns(grouped_first[:, 0:8], 3 * QC)
        quantize_columns(grouped_first[:, 8:QC], 3 * QC + 8)
        quantize_x(0, 0)

        later = []

        def add_quarter(q, a, b, engine_a="vector"):
            later.append((None, lambda: scale_quarter(q, 0, G)))
            later.append((None, lambda: permute_columns(grouped_half, QC * q, 8, 0, G)))
            later.append((None, lambda: permute_x(a[0], a[1], engine_a)))
            later.append((None, lambda: quantize_columns(grouped_half[:], QC * q)))
            later.append((("permuted", q), lambda: permute_columns(grouped_half, QC * q + 8, 8, 0, G)))
            later.append((None, lambda: permute_x(b[0], b[1], "vector")))
            later.append((("quarter", q), lambda: quantize_columns(grouped_half[:], QC * q + 8)))
            later.append((("x", a), lambda: quantize_x(a[0], a[1])))
            later.append((("x", b), lambda: quantize_x(b[0], b[1])))

        def add_x_pair(a, b, engine):
            later.append((None, lambda: permute_x(a[0], a[1], engine)))
            later.append((None, lambda: permute_x(b[0], b[1], engine)))
            later.append((("x", a), lambda: quantize_x(a[0], a[1])))
            later.append((("x", b), lambda: quantize_x(b[0], b[1])))

        later.append((("x", (0, 1)), lambda: quantize_x(0, 1)))
        add_quarter(2, (1, 0), (1, 1), "scalar")
        add_quarter(1, (2, 0), (3, 0))
        add_x_pair((2, 1), (3, 1), "vector")
        add_quarter(0, (4, 0), (4, 1))
        done = set()

        def need(what):
            while what not in done:
                key, call = later[len(done)]
                call()
                done.add((len(done), key) if key is None else key)

        NEEDS = {1: (("x", (0, 1)),), 2: (("quarter", 2), ("x", (1, 0))), 3: (("x", (1, 1)),), 4: (("quarter", 1), ("x", (3, 0))),
                 5: (("x", (3, 1)),), 6: (("permuted", 0),), 8: (("quarter", 0), ("x", (4, 1)))}

        out_tiles = {}
        for k, (groups, h, finished) in enumerate(STAGES):
            for what in NEEDS.get(k, ()):
                need(what)
            n = 0
            for grp in groups:
                piece = GROUP_PIECE[grp]
                line0, lines = PIECES[piece]
                if (piece, h) not in out_tiles:
                    out_tiles[(piece, h)] = big.tile([P, HB, 4 * lines], F32, name="o%d%d" % (piece, h), align_bytes=64,
                                                     offset=PIECE_OFFSETS[piece][h])
                ot = out_tiles[(piece, h)]
                xc, xsc = x_ready[(X_TILE_OF_GROUP[grp], h)]
                for line, step, count, first_slot, passes in JOBS[grp]:
                    pt = psum.tile([P, 512], F32, name="pt")
                    for f, (c, r, shift) in enumerate(passes):
                        nc.tensor.matmul_mx(
                            out=pt[:, 128 * f - HB * shift:128 * (f + 1) - HB * shift],
                            lhsT=psi_codes[:, c, :].bitcast(FP8X4),
                            lhsT_scale=psi_scl[:, c, :],
                            rhs=xc[:, 128 * r:128 * (r + 1)].bitcast(FP8X4),
                            rhs_scale=xsc[:, 128 * r:128 * (r + 1)],
                            start=True,
                            stop=True,
                        )
                    src = pt[:].rearrange("p (f j b) -> p b j f", f=4, j=4)[:, :, first_slot:first_slot + count, :]
                    n0 = line - line0
                    dst = ot[:].rearrange("p b (n f) -> p b n f", f=4)[:, :, n0:n0 + step * (count - 1) + 1:step, :]
                    if k in VECTOR_SHARES and (n % 2 == 1 or (k == 0 and n == 0)):
                        nc.vector.tensor_scalar(out=dst, in0=src, scalar1=OUT_SCALE, scalar2=None, op0=MULT)
                    else:
                        nc.scalar.activation(out=dst, in_=src, func=COPY, scale=OUT_SCALE)
                    n += 1
            if finished is not None:
                line0, lines = PIECES[finished]
                nc.sync.dma_start(out=out[:, HB * h:HB * (h + 1), 4 * line0:4 * (line0 + lines)], in_=out_tiles[(finished, h)][:])
